import numpy as np
import ml_dtypes


def mxq(x, axis, fmt="e4m3"):
    dtype, down = {"e4m3": (ml_dtypes.float8_e4m3fn, 7), "e5m2": (ml_dtypes.float8_e5m2, 14)}[fmt]
    v = np.moveaxis(np.asarray(x, np.float32).astype(ml_dtypes.bfloat16).astype(np.float64), axis, -1)
    blocks = v.reshape(v.shape[:-1] + (-1, 32))
    amax = np.abs(blocks).max(-1, keepdims=True)
    byte = np.maximum(np.where(amax > 0, np.frexp(amax)[1] - 1 + 127, 0) - down, 1)
    scale = np.exp2(byte - 127.0)
    codes = (blocks / scale).astype(np.float32).astype(dtype).astype(np.float64)
    return np.moveaxis((codes * scale).reshape(v.shape), -1, axis)


WIDE = False


def mx_kscale(k):
    if not WIDE:
        return np.ones(k)
    levels = np.array([10, -10, 5, -5, 0])
    a = np.random.permutation(np.resize(levels, k // 512 * 4)).reshape(k // 512, 4)
    idx = np.arange(k)
    return np.exp2(a[idx // 512, idx % 128 // 32])


BF16 = ml_dtypes.bfloat16


def bf(x):
    return np.asarray(x, np.float32).astype(BF16)


def f64(x):
    return np.asarray(x).astype(np.float64)


B, T, N, D, H, F = 2, 512, 4, 512, 8, 1024
S = B * N
EPS = 1e-5


def layernorm(v, g, b):
    mu = v.mean(-1, keepdims=True)
    var = np.square(v - mu).mean(-1, keepdims=True)
    return (v - mu) / np.sqrt(var + EPS) * g + b


def setup_inputs():
    s = mx_kscale(D)
    t = mx_kscale(D)
    return {"ax_cat": bf(np.random.standard_normal((S, T, D)) * 4.0 * s),
            "features": bf(np.random.standard_normal((B, T, N, D))),
            "wout_w": bf(np.random.standard_normal((D, D)) * 0.5 / np.sqrt(D) / s),
            "ln_g": bf((1.0 + 0.1 * np.random.standard_normal(D)) * t),
            "ln_b": bf(0.1 * np.random.standard_normal(D) * t),
            "ff1_w": bf(np.random.standard_normal((F, D)) / np.sqrt(D) / t),
            "ff1_b": bf(0.1 * np.random.standard_normal(F))}


def reference(ax_cat, features, wout_w, ln_g, ln_b, ff1_w, ff1_b):
    x = f64(features).transpose(0, 2, 1, 3).reshape(S, T, D)
    y = mxq(f64(ax_cat), 2, "e4m3") @ mxq(f64(wout_w), 1, "e4m3").T
    m = layernorm(y + x, f64(ln_g), f64(ln_b))
    return np.maximum((mxq(m, 2, "e4m3") @ mxq(f64(ff1_w), 1, "e4m3").T) + f64(ff1_b), 0.0)

@@ -1,0 +1,256 @@
+import math
+from contextlib import ExitStack
+
+import concourse.mybir as mybir
+from concourse.masks import make_identity
+
+F32 = mybir.dt.float32
+BF16 = mybir.dt.bfloat16
+U32 = mybir.dt.uint32
+U8 = mybir.dt.uint8
+FP8X4 = mybir.dt.float8_e4m3fn_x4
+ALU = mybir.AluOpType
+ACT = mybir.ActivationFunctionType
+
+P = 128
+PACK = 4
+BATCH, NODES = 2, 4
+SEQS = BATCH * NODES
+T = 512
+TILES = T // P
+D = 512
+F = 1024
+BANK = 512
+EPS = 1e-5
+
+FLOPS = 2 * SEQS * T * D * (D + F)
+
+
+def tile_temporalatt_pb_t_kernel(tc, ax_cat, features, wout_w, ln_g, ln_b, ff1_w, ff1_b, out):
+    nc = tc.nc
+    with ExitStack() as stack:
+        const = stack.enter_context(tc.tile_pool(name="const", bufs=1))
+        inputs = stack.enter_context(tc.tile_pool(name="inputs", bufs=1))
+        work = stack.enter_context(tc.tile_pool(name="work", bufs=2))
+        stats = stack.enter_context(tc.tile_pool(name="stats", bufs=3))
+        results = stack.enter_context(tc.tile_pool(name="results", bufs=3))
+        ps_norm = stack.enter_context(tc.psum_pool(name="ps_norm", bufs=4))
+        ps_main = stack.enter_context(tc.psum_pool(name="ps_main", bufs=4))
+
+        wout_sb = const.tile([P, D // P, D], BF16)
+        nc.sync.dma_start(out=wout_sb[:], in_=wout_w.rearrange("(o p) k -> p o k", p=P))
+        ax_sb = {}
+        x_sb = {}
+
+        def load_sequence(s):
+            ax_tile = inputs.tile([P, TILES, D], BF16, name="ax%d" % s)
+            nc.sync.dma_start(out=ax_tile[:], in_=ax_cat[s].rearrange("(p j) d -> p j d", j=TILES))
+            x_tile = inputs.tile([P, TILES, D], BF16, name="x%d" % s)
+            x_view = features[s // NODES].rearrange("(p j) n d -> p j n d", j=TILES)
+            nc.sync.dma_start(out=x_tile[:], in_=x_view[:, :, s % NODES, :])
+            ax_sb[s] = ax_tile
+            x_sb[s] = x_tile
+
+        load_sequence(0)
+
+        vector_rows = const.tile([P, P], BF16)
+        nc.vector.memset(vector_rows[:], 0.0)
+        nc.sync.dma_start(out=vector_rows[0:PACK, :], in_=ln_g.rearrange("(c k) -> c k", c=PACK))
+        nc.sync.dma_start(out=vector_rows[PACK : 2 * PACK, :], in_=ln_b.rearrange("(c k) -> c k", c=PACK))
+        bias_row = const.tile([P, F], BF16)
+        nc.vector.memset(bias_row[:], 0.0)
+        nc.sync.dma_start(out=bias_row[0:1, :], in_=ff1_b.rearrange("(o f) -> o f", o=1))
+        ff1_sb = const.tile([P, F // P, D], BF16)
+        nc.sync.dma_start(out=ff1_sb[:], in_=ff1_w.rearrange("(o p) k -> p o k", p=P))
+        for s in range(1, SEQS):
+            load_sequence(s)
+
+        ident_f32 = const.tile([P, P], F32)
+        make_identity(nc, ident_f32[:])
+        ident_bf16 = const.tile([P, P], BF16)
+        make_identity(nc, ident_bf16[:])
+        ones = const.tile([P, P], BF16)
+        nc.vector.memset(ones[:], 1.0)
+        eps = const.tile([P, 1], F32)
+        nc.vector.memset(eps[:], EPS)
+        warm = const.tile([P, 1], F32)
+        nc.scalar.activation(out=warm[:], in_=eps[:], func=ACT.Sqrt)
+
+        def quantise_rows(rows_sb, codes, scales):
+            grouped = work.tile([P, PACK * P, PACK], BF16, tag="grouped_rows", align_bytes=64)
+            grouped_words = grouped[:].bitcast(F32)
+            for half in range(2):
+                bank = ps_main.tile([P, 2, 2, P], F32, tag="main")
+                for i in range(2):
+                    words = rows_sb[:, 2 * half + i, :].bitcast(F32)
+                    for u in range(2):
+                        nc.tensor.transpose(bank[:, i, u, :], words[:, u * P : (u + 1) * P], ident_f32[:])
+                nc.scalar.copy(
+                    out=grouped_words[:, half * 2 * P : (half + 1) * 2 * P, :].rearrange("p (i r) u -> p i r u", i=2),
+                    in_=bank[:].rearrange("p i u r -> p i r u"),
+                )
+            nc.vector.quantize_mx(
+                out=codes.bitcast(FP8X4), scales=scales, in_=grouped[:].rearrange("p r t -> p (r t)")
+            )
+
+        wout_codes = const.tile([P, D], U32, align_bytes=64)
+        wout_scales = const.tile([P, D], U8, align_bytes=64)
+        quantise_rows(wout_sb, wout_codes[:], wout_scales[:])
+
+        vector_bank = ps_main.tile([P, P], BF16, tag="main")
+        nc.tensor.transpose(vector_bank[:], vector_rows[:], ident_bf16[:])
+        affine = const.tile([P, 2 * PACK], F32)
+        nc.vector.tensor_copy(out=affine[:], in_=vector_bank[:, 0 : 2 * PACK])
+
+        bias_all = const.tile([P, F], F32)
+        for h in range(F // BANK):
+            bias_bank = ps_main.tile([P, BANK], F32, tag="main")
+            nc.tensor.matmul(
+                out=bias_bank[:], lhsT=ones[:], rhs=bias_row[:, h * BANK : (h + 1) * BANK], start=True, stop=True
+            )
+            nc.vector.tensor_copy(out=bias_all[:, h * BANK : (h + 1) * BANK], in_=bias_bank[:])
+
+        ff1_grouped = const.tile([P, F, PACK], BF16, align_bytes=64)
+        for pair in range(F // (2 * P)):
+            bank = ps_main.tile([P, 2, PACK, P], BF16, tag="main")
+            for i in range(2):
+                for c in range(PACK):
+                    nc.tensor.transpose(bank[:, i, c, :], ff1_sb[:, 2 * pair + i, c * P : (c + 1) * P], ident_bf16[:])
+            nc.vector.tensor_copy(
+                out=ff1_grouped[:, pair * 2 * P : (pair + 1) * 2 * P, :].rearrange("p (i f) c -> p i f c", i=2),
+                in_=bank[:].rearrange("p i c f -> p i f c"),
+            )
+        ff1_codes = const.tile([P, F], U32, align_bytes=64)
+        ff1_scales = const.tile([P, F], U8, align_bytes=64)
+        nc.vector.quantize_mx(
+            out=ff1_codes[:].bitcast(FP8X4), scales=ff1_scales[:], in_=ff1_grouped[:].rearrange("p f c -> p (f c)")
+        )
+
+        ax_codes = {}
+        ax_scales = {}
+        normed = {}
+        m_codes = {}
+        m_scales = {}
+
+        def quantise_ax(s):
+            codes = work.tile([P, T], U32, tag="ax_codes", bufs=3, align_bytes=64)
+            scales = work.tile([P, T], U8, tag="ax_scales", bufs=3, align_bytes=64)
+            quantise_rows(ax_sb[s], codes[:], scales[:])
+            ax_codes[s] = codes
+            ax_scales[s] = scales
+
+        def project_and_normalise(s):
+            r = work.tile([P, TILES, D], F32, tag="r", bufs=3)
+            sums = stats.tile([P, TILES], F32, tag="sums")
+            for j in range(TILES):
+                y = ps_main.tile([P, D], F32, tag="main")
+                nc.tensor.matmul_mx(
+                    out=y[:],
+                    lhsT=ax_codes[s][:, j * P : (j + 1) * P].bitcast(FP8X4),
+                    lhsT_scale=ax_scales[s][:, j * P : (j + 1) * P],
+                    rhs=wout_codes[:].bitcast(FP8X4),
+                    rhs_scale=wout_scales[:],
+                    start=True,
+                    stop=True,
+                )
+                nc.vector.scalar_tensor_tensor(
+                    out=r[:, j, :],
+                    in0=y[:],
+                    scalar=1.0,
+                    in1=x_sb[s][:, j, :],
+                    op0=ALU.mult,
+                    op1=ALU.add,
+                    accum_out=sums[:, j : j + 1],
+                )
+            neg_mean = stats.tile([P, TILES], F32, tag="neg_mean")
+            nc.scalar.mul(out=neg_mean[:], in_=sums[:], mul=-1.0 / D)
+            squares = work.tile([P, TILES, D], BF16, tag="squares", bufs=1)
+            sum_sq = stats.tile([P, TILES], F32, tag="sum_sq")
+            for j in range(TILES):
+                nc.scalar.activation(
+                    out=squares[:, j, :],
+                    in_=r[:, j, :],
+                    func=ACT.Square,
+                    bias=neg_mean[:, j : j + 1],
+                    scale=1.0,
+                    accum_out=sum_sq[:, j : j + 1],
+                )
+            std = stats.tile([P, TILES], F32, tag="std")
+            nc.scalar.activation(out=std[:], in_=sum_sq[:], func=ACT.Sqrt, bias=eps[:], scale=1.0 / D)
+            rstd = stats.tile([P, TILES], F32, tag="rstd")
+            nc.vector.reciprocal(out=rstd[:], in_=std[:])
+            shift = stats.tile([P, TILES], F32, tag="shift")
+            nc.vector.tensor_mul(out=shift[:], in0=neg_mean[:], in1=rstd[:])
+            for j in range(TILES):
+                nc.scalar.activation(
+                    out=r[:, j, :],
+                    in_=r[:, j, :],
+                    func=ACT.Identity,
+                    bias=shift[:, j : j + 1],
+                    scale=rstd[:, j : j + 1],
+                )
+            normed[s] = r
+
+        def quantise_m(s):
+            planes = work.tile([P, PACK, T], BF16, tag="planes")
+            for c in range(PACK):
+                bank = ps_norm.tile([P, TILES, P], F32, tag="norm")
+                for j in range(TILES):
+                    nc.tensor.transpose(bank[:, j, :], normed[s][:, j, c * P : (c + 1) * P], ident_f32[:])
+                nc.scalar.activation(
+                    out=planes[:, c, :],
+                    in_=bank[:].rearrange("p j t -> p (j t)"),
+                    func=ACT.Identity,
+                    bias=affine[:, PACK + c : PACK + c + 1],
+                    scale=affine[:, c : c + 1],
+                )
+            grouped = work.tile([P, T, PACK], BF16, tag="grouped_m", align_bytes=64)
+            nc.vector.tensor_copy(
+                out=grouped[:].rearrange("p (w i) c -> p w c i", i=4),
+                in_=planes[:].rearrange("p c (w i) -> p w c i", i=4),
+            )
+            codes = work.tile([P, T], U32, tag="m_codes", align_bytes=64)
+            scales = work.tile([P, T], U8, tag="m_scales", align_bytes=64)
+            nc.vector.quantize_mx(
+                out=codes[:].bitcast(FP8X4), scales=scales[:], in_=grouped[:].rearrange("p t c -> p (t c)")
+            )
+            m_codes[s] = codes
+            m_scales[s] = scales
+
+        def feed_forward(s):
+            result = results.tile([P, TILES, F], F32, tag="result")
+            out_view = out[s].rearrange("(p j) f -> p j f", j=TILES)
+            for j in range(TILES):
+                for h in range(F // BANK):
+                    acc = ps_main.tile([P, BANK], F32, tag="main")
+                    nc.tensor.matmul_mx(
+                        out=acc[:],
+                        lhsT=m_codes[s][:, j * P : (j + 1) * P].bitcast(FP8X4),
+                        lhsT_scale=m_scales[s][:, j * P : (j + 1) * P],
+                        rhs=ff1_codes[:, h * BANK : (h + 1) * BANK].bitcast(FP8X4),
+                        rhs_scale=ff1_scales[:, h * BANK : (h + 1) * BANK],
+                        start=True,
+                        stop=True,
+                    )
+                    nc.vector.tensor_tensor(
+                        out=result[:, j, h * BANK : (h + 1) * BANK],
+                        in0=acc[:],
+                        in1=bias_all[:, h * BANK : (h + 1) * BANK],
+                        op=ALU.add,
+                    )
+                nc.gpsimd.tensor_scalar(
+                    out=result[:, j, :], in0=result[:, j, :], scalar1=math.inf, scalar2=0.0, op0=ALU.min, op1=ALU.max
+                )
+                if j % 2 == 1:
+                    nc.sync.dma_start(out=out_view[:, j - 1 : j + 1, :], in_=result[:, j - 1 : j + 1, :])
+
+        quantise_ax(0)
+        project_and_normalise(0)
+        quantise_ax(1)
+        for s in range(SEQS):
+            quantise_m(s)
+            if s + 1 < SEQS:
+                project_and_normalise(s + 1)
+            if s + 2 < SEQS:
+                quantise_ax(s + 2)
+            feed_forward(s)

@@ -29,13 +29,25 @@ FLOPS = 2 * SEQS * T * D * (D + F)
 def tile_temporalatt_pb_t_kernel(tc, ax_cat, features, wout_w, ln_g, ln_b, ff1_w, ff1_b, out):
     nc = tc.nc
     with ExitStack() as stack:
+        stack.enter_context(tc.manual_schedule())
         const = stack.enter_context(tc.tile_pool(name="const", bufs=1))
         inputs = stack.enter_context(tc.tile_pool(name="inputs", bufs=1))
         work = stack.enter_context(tc.tile_pool(name="work", bufs=2))
-        stats = stack.enter_context(tc.tile_pool(name="stats", bufs=3))
+        stats = stack.enter_context(tc.tile_pool(name="stats", bufs=2))
         results = stack.enter_context(tc.tile_pool(name="results", bufs=3))
-        ps_norm = stack.enter_context(tc.psum_pool(name="ps_norm", bufs=4))
-        ps_main = stack.enter_context(tc.psum_pool(name="ps_main", bufs=4))
+        ps_t = stack.enter_context(tc.psum_pool(name="ps_t", bufs=4))
+        ps_mx = stack.enter_context(tc.psum_pool(name="ps_mx", bufs=4))
+
+        ident_f32 = const.tile([P, P], F32)
+        make_identity(nc, ident_f32[:])
+        ident_bf16 = const.tile([P, P], BF16)
+        make_identity(nc, ident_bf16[:])
+        ones = const.tile([P, P], BF16)
+        nc.vector.memset(ones[:], 1.0)
+        eps = const.tile([P, 1], F32)
+        nc.vector.memset(eps[:], EPS)
+        warm = const.tile([P, 1], F32)
+        nc.scalar.activation(out=warm[:], in_=eps[:], func=ACT.Sqrt)
 
         wout_sb = const.tile([P, D // P, D], BF16)
         nc.sync.dma_start(out=wout_sb[:], in_=wout_w.rearrange("(o p) k -> p o k", p=P))
@@ -52,7 +64,6 @@ def tile_temporalatt_pb_t_kernel(tc, ax_cat, features, wout_w, ln_g, ln_b, ff1_w
             x_sb[s] = x_tile
 
         load_sequence(0)
-
         vector_rows = const.tile([P, P], BF16)
         nc.vector.memset(vector_rows[:], 0.0)
         nc.sync.dma_start(out=vector_rows[0:PACK, :], in_=ln_g.rearrange("(c k) -> c k", c=PACK))
@@ -65,22 +76,11 @@ def tile_temporalatt_pb_t_kernel(tc, ax_cat, features, wout_w, ln_g, ln_b, ff1_w
         for s in range(1, SEQS):
             load_sequence(s)
 
-        ident_f32 = const.tile([P, P], F32)
-        make_identity(nc, ident_f32[:])
-        ident_bf16 = const.tile([P, P], BF16)
-        make_identity(nc, ident_bf16[:])
-        ones = const.tile([P, P], BF16)
-        nc.vector.memset(ones[:], 1.0)
-        eps = const.tile([P, 1], F32)
-        nc.vector.memset(eps[:], EPS)
-        warm = const.tile([P, 1], F32)
-        nc.scalar.activation(out=warm[:], in_=eps[:], func=ACT.Sqrt)
-
-        def quantise_rows(rows_sb, codes, scales):
+        def transpose_rows(rows_sb):
             grouped = work.tile([P, PACK * P, PACK], BF16, tag="grouped_rows", align_bytes=64)
             grouped_words = grouped[:].bitcast(F32)
             for half in range(2):
-                bank = ps_main.tile([P, 2, 2, P], F32, tag="main")
+                bank = ps_t.tile([P, 2, 2, P], F32, tag="t")
                 for i in range(2):
                     words = rows_sb[:, 2 * half + i, :].bitcast(F32)
                     for u in range(2):
@@ -89,61 +89,76 @@ def tile_temporalatt_pb_t_kernel(tc, ax_cat, features, wout_w, ln_g, ln_b, ff1_w
                     out=grouped_words[:, half * 2 * P : (half + 1) * 2 * P, :].rearrange("p (i r) u -> p i r u", i=2),
                     in_=bank[:].rearrange("p i u r -> p i r u"),
                 )
+            return grouped
+
+        def quantise(grouped, codes, scales):
             nc.vector.quantize_mx(
-                out=codes.bitcast(FP8X4), scales=scales, in_=grouped[:].rearrange("p r t -> p (r t)")
+                out=codes[:].bitcast(FP8X4), scales=scales[:], in_=grouped[:].rearrange("p r t -> p (r t)")
             )
 
         wout_codes = const.tile([P, D], U32, align_bytes=64)
         wout_scales = const.tile([P, D], U8, align_bytes=64)
-        quantise_rows(wout_sb, wout_codes[:], wout_scales[:])
+        wout_grouped = transpose_rows(wout_sb)
+        quantise(wout_grouped, wout_codes, wout_scales)
 
-        vector_bank = ps_main.tile([P, P], BF16, tag="main")
-        nc.tensor.transpose(vector_bank[:], vector_rows[:], ident_bf16[:])
         affine = const.tile([P, 2 * PACK], F32)
-        nc.vector.tensor_copy(out=affine[:], in_=vector_bank[:, 0 : 2 * PACK])
-
         bias_all = const.tile([P, F], F32)
-        for h in range(F // BANK):
-            bias_bank = ps_main.tile([P, BANK], F32, tag="main")
-            nc.tensor.matmul(
-                out=bias_bank[:], lhsT=ones[:], rhs=bias_row[:, h * BANK : (h + 1) * BANK], start=True, stop=True
-            )
-            nc.vector.tensor_copy(out=bias_all[:, h * BANK : (h + 1) * BANK], in_=bias_bank[:])
-
         ff1_grouped = const.tile([P, F, PACK], BF16, align_bytes=64)
-        for pair in range(F // (2 * P)):
-            bank = ps_main.tile([P, 2, PACK, P], BF16, tag="main")
-            for i in range(2):
-                for c in range(PACK):
-                    nc.tensor.transpose(bank[:, i, c, :], ff1_sb[:, 2 * pair + i, c * P : (c + 1) * P], ident_bf16[:])
-            nc.vector.tensor_copy(
-                out=ff1_grouped[:, pair * 2 * P : (pair + 1) * 2 * P, :].rearrange("p (i f) c -> p i f c", i=2),
-                in_=bank[:].rearrange("p i c f -> p i f c"),
-            )
         ff1_codes = const.tile([P, F], U32, align_bytes=64)
         ff1_scales = const.tile([P, F], U8, align_bytes=64)
-        nc.vector.quantize_mx(
-            out=ff1_codes[:].bitcast(FP8X4), scales=ff1_scales[:], in_=ff1_grouped[:].rearrange("p f c -> p (f c)")
-        )
 
+        def prepare_second_layer():
+            vector_bank = ps_t.tile([P, P], BF16, tag="t")
+            nc.tensor.transpose(vector_bank[:], vector_rows[:], ident_bf16[:])
+            nc.vector.tensor_copy(out=affine[:], in_=vector_bank[:, 0 : 2 * PACK])
+            for pair in range(F // (2 * P)):
+                bank = ps_t.tile([P, 2, PACK, P], BF16, tag="t")
+                for i in range(2):
+                    for c in range(PACK):
+                        nc.tensor.transpose(
+                            bank[:, i, c, :], ff1_sb[:, 2 * pair + i, c * P : (c + 1) * P], ident_bf16[:]
+                        )
+                nc.vector.tensor_copy(
+                    out=ff1_grouped[:, pair * 2 * P : (pair + 1) * 2 * P, :].rearrange("p (i f) c -> p i f c", i=2),
+                    in_=bank[:].rearrange("p i c f -> p i f c"),
+                )
+            quantise(ff1_grouped, ff1_codes, ff1_scales)
+            for h in range(F // BANK):
+                bias_bank = ps_mx.tile([P, BANK], F32, tag="mx")
+                nc.tensor.matmul(
+                    out=bias_bank[:], lhsT=ones[:], rhs=bias_row[:, h * BANK : (h + 1) * BANK], start=True, stop=True
+                )
+                nc.vector.tensor_copy(out=bias_all[:, h * BANK : (h + 1) * BANK], in_=bias_bank[:])
+
+        ax_grouped = {}
         ax_codes = {}
         ax_scales = {}
-        normed = {}
+        residual = {}
+        row_sum = {}
+        neg_mean = {}
+        std = {}
+        rstd = {}
+        shift = {}
+        m_planes = {}
         m_codes = {}
         m_scales = {}
+        result = {}
 
-        def quantise_ax(s):
-            codes = work.tile([P, T], U32, tag="ax_codes", bufs=3, align_bytes=64)
-            scales = work.tile([P, T], U8, tag="ax_scales", bufs=3, align_bytes=64)
-            quantise_rows(ax_sb[s], codes[:], scales[:])
+        def ax_transpose(s):
+            ax_grouped[s] = transpose_rows(ax_sb[s])
+
+        def ax_quantise(s):
+            codes = work.tile([P, T], U32, tag="ax_codes", align_bytes=64)
+            scales = work.tile([P, T], U8, tag="ax_scales", align_bytes=64)
+            quantise(ax_grouped[s], codes, scales)
             ax_codes[s] = codes
             ax_scales[s] = scales
 
-        def project_and_normalise(s):
+        def project(s):
             r = work.tile([P, TILES, D], F32, tag="r", bufs=3)
             sums = stats.tile([P, TILES], F32, tag="sums")
             for j in range(TILES):
-                y = ps_main.tile([P, D], F32, tag="main")
+                y = ps_mx.tile([P, D], F32, tag="mx")
                 nc.tensor.matmul_mx(
                     out=y[:],
                     lhsT=ax_codes[s][:, j * P : (j + 1) * P].bitcast(FP8X4),
@@ -162,41 +177,52 @@ def tile_temporalatt_pb_t_kernel(tc, ax_cat, features, wout_w, ln_g, ln_b, ff1_w
                     op1=ALU.add,
                     accum_out=sums[:, j : j + 1],
                 )
-            neg_mean = stats.tile([P, TILES], F32, tag="neg_mean")
-            nc.scalar.mul(out=neg_mean[:], in_=sums[:], mul=-1.0 / D)
+            residual[s] = r
+            row_sum[s] = sums
+
+        def statistics(s):
+            minus = stats.tile([P, TILES], F32, tag="neg_mean")
+            nc.scalar.mul(out=minus[:], in_=row_sum[s][:], mul=-1.0 / D)
             squares = work.tile([P, TILES, D], BF16, tag="squares", bufs=1)
             sum_sq = stats.tile([P, TILES], F32, tag="sum_sq")
             for j in range(TILES):
                 nc.scalar.activation(
                     out=squares[:, j, :],
-                    in_=r[:, j, :],
+                    in_=residual[s][:, j, :],
                     func=ACT.Square,
-                    bias=neg_mean[:, j : j + 1],
+                    bias=minus[:, j : j + 1],
                     scale=1.0,
                     accum_out=sum_sq[:, j : j + 1],
                 )
-            std = stats.tile([P, TILES], F32, tag="std")
-            nc.scalar.activation(out=std[:], in_=sum_sq[:], func=ACT.Sqrt, bias=eps[:], scale=1.0 / D)
-            rstd = stats.tile([P, TILES], F32, tag="rstd")
-            nc.vector.reciprocal(out=rstd[:], in_=std[:])
-            shift = stats.tile([P, TILES], F32, tag="shift")
-            nc.vector.tensor_mul(out=shift[:], in0=neg_mean[:], in1=rstd[:])
+            root = stats.tile([P, TILES], F32, tag="std")
+            nc.scalar.activation(out=root[:], in_=sum_sq[:], func=ACT.Sqrt, bias=eps[:], scale=1.0 / D)
+            neg_mean[s] = minus
+            std[s] = root
+
+        def inverse_std(s):
+            inverse = stats.tile([P, TILES], F32, tag="rstd")
+            nc.vector.reciprocal(out=inverse[:], in_=std[s][:])
+            offset = stats.tile([P, TILES], F32, tag="shift")
+            nc.vector.tensor_mul(out=offset[:], in0=neg_mean[s][:], in1=inverse[:])
+            rstd[s] = inverse
+            shift[s] = offset
+
+        def normalise(s):
             for j in range(TILES):
                 nc.scalar.activation(
-                    out=r[:, j, :],
-                    in_=r[:, j, :],
+                    out=residual[s][:, j, :],
+                    in_=residual[s][:, j, :],
                     func=ACT.Identity,
-                    bias=shift[:, j : j + 1],
-                    scale=rstd[:, j : j + 1],
+                    bias=shift[s][:, j : j + 1],
+                    scale=rstd[s][:, j : j + 1],
                 )
-            normed[s] = r
 
-        def quantise_m(s):
+        def m_transpose(s):
             planes = work.tile([P, PACK, T], BF16, tag="planes")
             for c in range(PACK):
-                bank = ps_norm.tile([P, TILES, P], F32, tag="norm")
+                bank = ps_t.tile([P, TILES, P], F32, tag="t")
                 for j in range(TILES):
-                    nc.tensor.transpose(bank[:, j, :], normed[s][:, j, c * P : (c + 1) * P], ident_f32[:])
+                    nc.tensor.transpose(bank[:, j, :], residual[s][:, j, c * P : (c + 1) * P], ident_f32[:])
                 nc.scalar.activation(
                     out=planes[:, c, :],
                     in_=bank[:].rearrange("p j t -> p (j t)"),
@@ -204,25 +230,24 @@ def tile_temporalatt_pb_t_kernel(tc, ax_cat, features, wout_w, ln_g, ln_b, ff1_w
                     bias=affine[:, PACK + c : PACK + c + 1],
                     scale=affine[:, c : c + 1],
                 )
+            m_planes[s] = planes
+
+        def m_quantise(s):
             grouped = work.tile([P, T, PACK], BF16, tag="grouped_m", align_bytes=64)
             nc.vector.tensor_copy(
                 out=grouped[:].rearrange("p (w i) c -> p w c i", i=4),
-                in_=planes[:].rearrange("p c (w i) -> p w c i", i=4),
+                in_=m_planes[s][:].rearrange("p c (w i) -> p w c i", i=4),
             )
             codes = work.tile([P, T], U32, tag="m_codes", align_bytes=64)
             scales = work.tile([P, T], U8, tag="m_scales", align_bytes=64)
-            nc.vector.quantize_mx(
-                out=codes[:].bitcast(FP8X4), scales=scales[:], in_=grouped[:].rearrange("p t c -> p (t c)")
-            )
+            quantise(grouped, codes, scales)
             m_codes[s] = codes
             m_scales[s] = scales
 
-        def feed_forward(s):
-            result = results.tile([P, TILES, F], F32, tag="result")
-            out_view = out[s].rearrange("(p j) f -> p j f", j=TILES)
-            for j in range(TILES):
+        def feed_forward(s, tiles):
+            for j in tiles:
                 for h in range(F // BANK):
-                    acc = ps_main.tile([P, BANK], F32, tag="main")
+                    acc = ps_mx.tile([P, BANK], F32, tag="mx")
                     nc.tensor.matmul_mx(
                         out=acc[:],
                         lhsT=m_codes[s][:, j * P : (j + 1) * P].bitcast(FP8X4),
@@ -233,24 +258,52 @@ def tile_temporalatt_pb_t_kernel(tc, ax_cat, features, wout_w, ln_g, ln_b, ff1_w
                         stop=True,
                     )
                     nc.vector.tensor_tensor(
-                        out=result[:, j, h * BANK : (h + 1) * BANK],
+                        out=result[s][:, j, h * BANK : (h + 1) * BANK],
                         in0=acc[:],
                         in1=bias_all[:, h * BANK : (h + 1) * BANK],
                         op=ALU.add,
                     )
-                nc.gpsimd.tensor_scalar(
-                    out=result[:, j, :], in0=result[:, j, :], scalar1=math.inf, scalar2=0.0, op0=ALU.min, op1=ALU.max
-                )
-                if j % 2 == 1:
-                    nc.sync.dma_start(out=out_view[:, j - 1 : j + 1, :], in_=result[:, j - 1 : j + 1, :])
 
-        quantise_ax(0)
-        project_and_normalise(0)
-        quantise_ax(1)
-        for s in range(SEQS):
-            quantise_m(s)
-            if s + 1 < SEQS:
-                project_and_normalise(s + 1)
-            if s + 2 < SEQS:
-                quantise_ax(s + 2)
-            feed_forward(s)
+        def relu_and_store(s):
+            out_view = out[s].rearrange("(p j) f -> p j f", j=TILES)
+            for j in range(0, TILES, 2):
+                nc.gpsimd.tensor_scalar(
+                    out=result[s][:, j : j + 2, :],
+                    in0=result[s][:, j : j + 2, :],
+                    scalar1=math.inf,
+                    scalar2=0.0,
+                    op0=ALU.min,
+                    op1=ALU.max,
+                )
+                nc.sync.dma_start(out=out_view[:, j : j + 2, :], in_=result[s][:, j : j + 2, :])
+
+        def live(s):
+            return 0 <= s < SEQS
+
+        for i in range(-5, SEQS + 1):
+            if live(i + 1):
+                m_transpose(i + 1)
+            if live(i + 5):
+                ax_transpose(i + 5)
+            if live(i + 4):
+                ax_quantise(i + 4)
+            if live(i):
+                m_quantise(i)
+            if live(i + 3):
+                project(i + 3)
+            if live(i + 2):
+                statistics(i + 2)
+            if live(i):
+                result_tile = results.tile([P, TILES, F], F32, tag="result")
+                result[i] = result_tile
+                feed_forward(i, (0,))
+            if live(i + 2):
+                inverse_std(i + 2)
+            if live(i - 1):
+                relu_and_store(i - 1)
+            if live(i):
+                feed_forward(i, (1, 2, 3))
+            if live(i + 2):
+                normalise(i + 2)
+            if i == -2:
+                prepare_second_layer()

@@ -1,4 +1,3 @@
-import math
 from contextlib import ExitStack
 
 import concourse.mybir as mybir
@@ -22,6 +21,7 @@ D = 512
 F = 1024
 BANK = 512
 EPS = 1e-5
+PREPARE_ROUND = -3
 
 FLOPS = 2 * SEQS * T * D * (D + F)
 
@@ -33,7 +33,7 @@ def tile_temporalatt_pb_t_kernel(tc, ax_cat, features, wout_w, ln_g, ln_b, ff1_w
         const = stack.enter_context(tc.tile_pool(name="const", bufs=1))
         inputs = stack.enter_context(tc.tile_pool(name="inputs", bufs=1))
         work = stack.enter_context(tc.tile_pool(name="work", bufs=2))
-        stats = stack.enter_context(tc.tile_pool(name="stats", bufs=2))
+        stats = stack.enter_context(tc.tile_pool(name="stats", bufs=3))
         results = stack.enter_context(tc.tile_pool(name="results", bufs=3))
         ps_t = stack.enter_context(tc.psum_pool(name="ps_t", bufs=4))
         ps_mx = stack.enter_context(tc.psum_pool(name="ps_mx", bufs=4))
@@ -110,7 +110,7 @@ def tile_temporalatt_pb_t_kernel(tc, ax_cat, features, wout_w, ln_g, ln_b, ff1_w
         def prepare_second_layer():
             vector_bank = ps_t.tile([P, P], BF16, tag="t")
             nc.tensor.transpose(vector_bank[:], vector_rows[:], ident_bf16[:])
-            nc.vector.tensor_copy(out=affine[:], in_=vector_bank[:, 0 : 2 * PACK])
+            nc.scalar.copy(out=affine[:], in_=vector_bank[:, 0 : 2 * PACK])
             for pair in range(F // (2 * P)):
                 bank = ps_t.tile([P, 2, PACK, P], BF16, tag="t")
                 for i in range(2):
@@ -118,7 +118,7 @@ def tile_temporalatt_pb_t_kernel(tc, ax_cat, features, wout_w, ln_g, ln_b, ff1_w
                         nc.tensor.transpose(
                             bank[:, i, c, :], ff1_sb[:, 2 * pair + i, c * P : (c + 1) * P], ident_bf16[:]
                         )
-                nc.vector.tensor_copy(
+                nc.scalar.copy(
                     out=ff1_grouped[:, pair * 2 * P : (pair + 1) * 2 * P, :].rearrange("p (i f) c -> p i f c", i=2),
                     in_=bank[:].rearrange("p i c f -> p i f c"),
                 )
@@ -128,7 +128,7 @@ def tile_temporalatt_pb_t_kernel(tc, ax_cat, features, wout_w, ln_g, ln_b, ff1_w
                 nc.tensor.matmul(
                     out=bias_bank[:], lhsT=ones[:], rhs=bias_row[:, h * BANK : (h + 1) * BANK], start=True, stop=True
                 )
-                nc.vector.tensor_copy(out=bias_all[:, h * BANK : (h + 1) * BANK], in_=bias_bank[:])
+                nc.scalar.copy(out=bias_all[:, h * BANK : (h + 1) * BANK], in_=bias_bank[:])
 
         ax_grouped = {}
         ax_codes = {}
@@ -138,11 +138,9 @@ def tile_temporalatt_pb_t_kernel(tc, ax_cat, features, wout_w, ln_g, ln_b, ff1_w
         neg_mean = {}
         std = {}
         rstd = {}
-        shift = {}
         m_planes = {}
         m_codes = {}
         m_scales = {}
-        result = {}
 
         def ax_transpose(s):
             ax_grouped[s] = transpose_rows(ax_sb[s])
@@ -155,7 +153,7 @@ def tile_temporalatt_pb_t_kernel(tc, ax_cat, features, wout_w, ln_g, ln_b, ff1_w
             ax_scales[s] = scales
 
         def project(s):
-            r = work.tile([P, TILES, D], F32, tag="r", bufs=3)
+            r = work.tile([P, TILES, D], F32, tag="r", bufs=4)
             sums = stats.tile([P, TILES], F32, tag="sums")
             for j in range(TILES):
                 y = ps_mx.tile([P, D], F32, tag="mx")
@@ -202,19 +200,17 @@ def tile_temporalatt_pb_t_kernel(tc, ax_cat, features, wout_w, ln_g, ln_b, ff1_w
         def inverse_std(s):
             inverse = stats.tile([P, TILES], F32, tag="rstd")
             nc.vector.reciprocal(out=inverse[:], in_=std[s][:])
-            offset = stats.tile([P, TILES], F32, tag="shift")
-            nc.vector.tensor_mul(out=offset[:], in0=neg_mean[s][:], in1=inverse[:])
             rstd[s] = inverse
-            shift[s] = offset
 
         def normalise(s):
             for j in range(TILES):
-                nc.scalar.activation(
+                nc.gpsimd.tensor_scalar(
                     out=residual[s][:, j, :],
-                    in_=residual[s][:, j, :],
-                    func=ACT.Identity,
-                    bias=shift[s][:, j : j + 1],
-                    scale=rstd[s][:, j : j + 1],
+                    in0=residual[s][:, j, :],
+                    scalar1=neg_mean[s][:, j : j + 1],
+                    scalar2=rstd[s][:, j : j + 1],
+                    op0=ALU.add,
+                    op1=ALU.mult,
                 )
 
         def m_transpose(s):
@@ -244,8 +240,10 @@ def tile_temporalatt_pb_t_kernel(tc, ax_cat, features, wout_w, ln_g, ln_b, ff1_w
             m_codes[s] = codes
             m_scales[s] = scales
 
-        def feed_forward(s, tiles):
-            for j in tiles:
+        def feed_forward(s):
+            result = results.tile([P, TILES, F], F32, tag="result")
+            out_view = out[s].rearrange("(p j) f -> p j f", j=TILES)
+            for j in range(TILES):
                 for h in range(F // BANK):
                     acc = ps_mx.tile([P, BANK], F32, tag="mx")
                     nc.tensor.matmul_mx(
@@ -258,52 +256,38 @@ def tile_temporalatt_pb_t_kernel(tc, ax_cat, features, wout_w, ln_g, ln_b, ff1_w
                         stop=True,
                     )
                     nc.vector.tensor_tensor(
-                        out=result[s][:, j, h * BANK : (h + 1) * BANK],
+                        out=result[:, j, h * BANK : (h + 1) * BANK],
                         in0=acc[:],
                         in1=bias_all[:, h * BANK : (h + 1) * BANK],
                         op=ALU.add,
                     )
-
-        def relu_and_store(s):
-            out_view = out[s].rearrange("(p j) f -> p j f", j=TILES)
-            for j in range(0, TILES, 2):
-                nc.gpsimd.tensor_scalar(
-                    out=result[s][:, j : j + 2, :],
-                    in0=result[s][:, j : j + 2, :],
-                    scalar1=math.inf,
-                    scalar2=0.0,
-                    op0=ALU.min,
-                    op1=ALU.max,
-                )
-                nc.sync.dma_start(out=out_view[:, j : j + 2, :], in_=result[s][:, j : j + 2, :])
+                if j < TILES - 1:
+                    nc.scalar.activation(out=result[:, j, :], in_=result[:, j, :], func=ACT.Relu)
+                else:
+                    nc.vector.tensor_scalar_max(out=result[:, j, :], in0=result[:, j, :], scalar1=0.0)
+                nc.sync.dma_start(out=out_view[:, j, :], in_=result[:, j, :])
 
         def live(s):
             return 0 <= s < SEQS
 
-        for i in range(-5, SEQS + 1):
+        for i in range(-6, SEQS):
+            if live(i + 2):
+                inverse_std(i + 2)
+            if live(i + 4):
+                project(i + 4)
             if live(i + 1):
                 m_transpose(i + 1)
+            if live(i + 6):
+                ax_transpose(i + 6)
+            if live(i + 2):
+                normalise(i + 2)
             if live(i + 5):
-                ax_transpose(i + 5)
-            if live(i + 4):
-                ax_quantise(i + 4)
+                ax_quantise(i + 5)
             if live(i):
                 m_quantise(i)
             if live(i + 3):
-                project(i + 3)
-            if live(i + 2):
-                statistics(i + 2)
-            if live(i):
-                result_tile = results.tile([P, TILES, F], F32, tag="result")
-                result[i] = result_tile
-                feed_forward(i, (0,))
-            if live(i + 2):
-                inverse_std(i + 2)
-            if live(i - 1):
-                relu_and_store(i - 1)
-            if live(i):
-                feed_forward(i, (1, 2, 3))
-            if live(i + 2):
-                normalise(i + 2)
-            if i == -2:
+                statistics(i + 3)
+            if i == PREPARE_ROUND:
                 prepare_second_layer()
+            if live(i):
+                feed_forward(i)

@@ -29,7 +29,6 @@ FLOPS = 2 * SEQS * T * D * (D + F)
 def tile_temporalatt_pb_t_kernel(tc, ax_cat, features, wout_w, ln_g, ln_b, ff1_w, ff1_b, out):
     nc = tc.nc
     with ExitStack() as stack:
-        stack.enter_context(tc.manual_schedule())
         const = stack.enter_context(tc.tile_pool(name="const", bufs=1))
         inputs = stack.enter_context(tc.tile_pool(name="inputs", bufs=1))
         work = stack.enter_context(tc.tile_pool(name="work", bufs=2))

@@ -1,3 +1,4 @@
+import math
 from contextlib import ExitStack
 
 import concourse.mybir as mybir
@@ -260,7 +261,16 @@ def tile_temporalatt_pb_t_kernel(tc, ax_cat, features, wout_w, ln_g, ln_b, ff1_w
                         in1=bias_all[:, h * BANK : (h + 1) * BANK],
                         op=ALU.add,
                     )
-                if j < TILES - 1:
+                if j == 0:
+                    nc.gpsimd.tensor_scalar(
+                        out=result[:, j, :],
+                        in0=result[:, j, :],
+                        scalar1=math.inf,
+                        scalar2=0.0,
+                        op0=ALU.min,
+                        op1=ALU.max,
+                    )
+                elif j < TILES - 1:
                     nc.scalar.activation(out=result[:, j, :], in_=result[:, j, :], func=ACT.Relu)
                 else:
                     nc.vector.tensor_scalar_max(out=result[:, j, :], in0=result[:, j, :], scalar1=0.0)

@@ -1,4 +1,3 @@
-import math
 from contextlib import ExitStack
 
 import concourse.mybir as mybir
@@ -85,7 +84,8 @@ def tile_temporalatt_pb_t_kernel(tc, ax_cat, features, wout_w, ln_g, ln_b, ff1_w
                     words = rows_sb[:, 2 * half + i, :].bitcast(F32)
                     for u in range(2):
                         nc.tensor.transpose(bank[:, i, u, :], words[:, u * P : (u + 1) * P], ident_f32[:])
-                nc.scalar.copy(
+                copy_out = nc.scalar.copy if half == 0 else nc.vector.tensor_copy
+                copy_out(
                     out=grouped_words[:, half * 2 * P : (half + 1) * 2 * P, :].rearrange("p (i r) u -> p i r u", i=2),
                     in_=bank[:].rearrange("p i u r -> p i r u"),
                 )
@@ -118,7 +118,8 @@ def tile_temporalatt_pb_t_kernel(tc, ax_cat, features, wout_w, ln_g, ln_b, ff1_w
                         nc.tensor.transpose(
                             bank[:, i, c, :], ff1_sb[:, 2 * pair + i, c * P : (c + 1) * P], ident_bf16[:]
                         )
-                nc.scalar.copy(
+                copy_out = nc.scalar.copy if pair % 2 == 0 else nc.vector.tensor_copy
+                copy_out(
                     out=ff1_grouped[:, pair * 2 * P : (pair + 1) * 2 * P, :].rearrange("p (i f) c -> p i f c", i=2),
                     in_=bank[:].rearrange("p i c f -> p i f c"),
                 )
@@ -261,19 +262,7 @@ def tile_temporalatt_pb_t_kernel(tc, ax_cat, features, wout_w, ln_g, ln_b, ff1_w
                         in1=bias_all[:, h * BANK : (h + 1) * BANK],
                         op=ALU.add,
                     )
-                if j == 0:
-                    nc.gpsimd.tensor_scalar(
-                        out=result[:, j, :],
-                        in0=result[:, j, :],
-                        scalar1=math.inf,
-                        scalar2=0.0,
-                        op0=ALU.min,
-                        op1=ALU.max,
-                    )
-                elif j < TILES - 1:
-                    nc.scalar.activation(out=result[:, j, :], in_=result[:, j, :], func=ACT.Relu)
-                else:
-                    nc.vector.tensor_scalar_max(out=result[:, j, :], in0=result[:, j, :], scalar1=0.0)
+                nc.scalar.activation(out=result[:, j, :], in_=result[:, j, :], func=ACT.Relu)
                 nc.sync.dma_start(out=out_view[:, j, :], in_=result[:, j, :])
 
         def live(s):

from contextlib import ExitStack

import concourse.mybir as mybir
from concourse.masks import make_identity

F32 = mybir.dt.float32
BF16 = mybir.dt.bfloat16
U32 = mybir.dt.uint32
U8 = mybir.dt.uint8
FP8X4 = mybir.dt.float8_e4m3fn_x4
ALU = mybir.AluOpType
ACT = mybir.ActivationFunctionType

P = 128
PACK = 4
BATCH, NODES = 2, 4
SEQS = BATCH * NODES
T = 512
TILES = T // P
D = 512
F = 1024
BANK = 512
EPS = 1e-5
PREPARE_ROUND = -3

FLOPS = 2 * SEQS * T * D * (D + F)


def tile_temporalatt_pb_t_kernel(tc, ax_cat, features, wout_w, ln_g, ln_b, ff1_w, ff1_b, out):
    nc = tc.nc
    with ExitStack() as stack:
        const = stack.enter_context(tc.tile_pool(name="const", bufs=1))
        inputs = stack.enter_context(tc.tile_pool(name="inputs", bufs=1))
        work = stack.enter_context(tc.tile_pool(name="work", bufs=2))
        stats = stack.enter_context(tc.tile_pool(name="stats", bufs=3))
        results = stack.enter_context(tc.tile_pool(name="results", bufs=3))
        ps_t = stack.enter_context(tc.psum_pool(name="ps_t", bufs=4))
        ps_mx = stack.enter_context(tc.psum_pool(name="ps_mx", bufs=4))

        ident_f32 = const.tile([P, P], F32)
        make_identity(nc, ident_f32[:])
        ident_bf16 = const.tile([P, P], BF16)
        make_identity(nc, ident_bf16[:])
        ones = const.tile([P, P], BF16)
        nc.vector.memset(ones[:], 1.0)
        eps = const.tile([P, 1], F32)
        nc.vector.memset(eps[:], EPS)
        warm = const.tile([P, 1], F32)
        nc.scalar.activation(out=warm[:], in_=eps[:], func=ACT.Sqrt)

        wout_sb = const.tile([P, D // P, D], BF16)
        nc.sync.dma_start(out=wout_sb[:], in_=wout_w.rearrange("(o p) k -> p o k", p=P))
        ax_sb = {}
        x_sb = {}

        def load_sequence(s):
            ax_tile = inputs.tile([P, TILES, D], BF16, name="ax%d" % s)
            nc.sync.dma_start(out=ax_tile[:], in_=ax_cat[s].rearrange("(p j) d -> p j d", j=TILES))
            x_tile = inputs.tile([P, TILES, D], BF16, name="x%d" % s)
            x_view = features[s // NODES].rearrange("(p j) n d -> p j n d", j=TILES)
            nc.sync.dma_start(out=x_tile[:], in_=x_view[:, :, s % NODES, :])
            ax_sb[s] = ax_tile
            x_sb[s] = x_tile

        load_sequence(0)
        vector_rows = const.tile([P, P], BF16)
        nc.vector.memset(vector_rows[:], 0.0)
        nc.sync.dma_start(out=vector_rows[0:PACK, :], in_=ln_g.rearrange("(c k) -> c k", c=PACK))
        nc.sync.dma_start(out=vector_rows[PACK : 2 * PACK, :], in_=ln_b.rearrange("(c k) -> c k", c=PACK))
        bias_row = const.tile([P, F], BF16)
        nc.vector.memset(bias_row[:], 0.0)
        nc.sync.dma_start(out=bias_row[0:1, :], in_=ff1_b.rearrange("(o f) -> o f", o=1))
        ff1_sb = const.tile([P, F // P, D], BF16)
        nc.sync.dma_start(out=ff1_sb[:], in_=ff1_w.rearrange("(o p) k -> p o k", p=P))
        for s in range(1, SEQS):
            load_sequence(s)

        def transpose_rows(rows_sb):
            grouped = work.tile([P, PACK * P, PACK], BF16, tag="grouped_rows", align_bytes=64)
            grouped_words = grouped[:].bitcast(F32)
            for half in range(2):
                bank = ps_t.tile([P, 2, 2, P], F32, tag="t")
                for i in range(2):
                    words = rows_sb[:, 2 * half + i, :].bitcast(F32)
                    for u in range(2):
                        nc.tensor.transpose(bank[:, i, u, :], words[:, u * P : (u + 1) * P], ident_f32[:])
                copy_out = nc.scalar.copy if half == 0 else nc.vector.tensor_copy
                copy_out(
                    out=grouped_words[:, half * 2 * P : (half + 1) * 2 * P, :].rearrange("p (i r) u -> p i r u", i=2),
                    in_=bank[:].rearrange("p i u r -> p i r u"),
                )
            return grouped

        def quantise(grouped, codes, scales):
            nc.vector.quantize_mx(
                out=codes[:].bitcast(FP8X4), scales=scales[:], in_=grouped[:].rearrange("p r t -> p (r t)")
            )

        wout_codes = const.tile([P, D], U32, align_bytes=64)
        wout_scales = const.tile([P, D], U8, align_bytes=64)
        wout_grouped = transpose_rows(wout_sb)
        quantise(wout_grouped, wout_codes, wout_scales)

        affine = const.tile([P, 2 * PACK], F32)
        bias_all = const.tile([P, F], F32)
        ff1_grouped = const.tile([P, F, PACK], BF16, align_bytes=64)
        ff1_codes = const.tile([P, F], U32, align_bytes=64)
        ff1_scales = const.tile([P, F], U8, align_bytes=64)

        def prepare_second_layer():
            vector_bank = ps_t.tile([P, P], BF16, tag="t")
            nc.tensor.transpose(vector_bank[:], vector_rows[:], ident_bf16[:])
            nc.scalar.copy(out=affine[:], in_=vector_bank[:, 0 : 2 * PACK])
            for pair in range(F // (2 * P)):
                bank = ps_t.tile([P, 2, PACK, P], BF16, tag="t")
                for i in range(2):
                    for c in range(PACK):
                        nc.tensor.transpose(
                            bank[:, i, c, :], ff1_sb[:, 2 * pair + i, c * P : (c + 1) * P], ident_bf16[:]
                        )
                copy_out = nc.scalar.copy if pair % 2 == 0 else nc.vector.tensor_copy
                copy_out(
                    out=ff1_grouped[:, pair * 2 * P : (pair + 1) * 2 * P, :].rearrange("p (i f) c -> p i f c", i=2),
                    in_=bank[:].rearrange("p i c f -> p i f c"),
                )
            quantise(ff1_grouped, ff1_codes, ff1_scales)
            for h in range(F // BANK):
                bias_bank = ps_mx.tile([P, BANK], F32, tag="mx")
                nc.tensor.matmul(
                    out=bias_bank[:], lhsT=ones[:], rhs=bias_row[:, h * BANK : (h + 1) * BANK], start=True, stop=True
                )
                nc.scalar.copy(out=bias_all[:, h * BANK : (h + 1) * BANK], in_=bias_bank[:])

        ax_grouped = {}
        ax_codes = {}
        ax_scales = {}
        residual = {}
        row_sum = {}
        neg_mean = {}
        std = {}
        rstd = {}
        m_planes = {}
        m_codes = {}
        m_scales = {}

        def ax_transpose(s):
            ax_grouped[s] = transpose_rows(ax_sb[s])

        def ax_quantise(s):
            codes = work.tile([P, T], U32, tag="ax_codes", align_bytes=64)
            scales = work.tile([P, T], U8, tag="ax_scales", align_bytes=64)
            quantise(ax_grouped[s], codes, scales)
            ax_codes[s] = codes
            ax_scales[s] = scales

        def project(s):
            r = work.tile([P, TILES, D], F32, tag="r", bufs=4)
            sums = stats.tile([P, TILES], F32, tag="sums")
            for j in range(TILES):
                y = ps_mx.tile([P, D], F32, tag="mx")
                nc.tensor.matmul_mx(
                    out=y[:],
                    lhsT=ax_codes[s][:, j * P : (j + 1) * P].bitcast(FP8X4),
                    lhsT_scale=ax_scales[s][:, j * P : (j + 1) * P],
                    rhs=wout_codes[:].bitcast(FP8X4),
                    rhs_scale=wout_scales[:],
                    start=True,
                    stop=True,
                )
                nc.vector.scalar_tensor_tensor(
                    out=r[:, j, :],
                    in0=y[:],
                    scalar=1.0,
                    in1=x_sb[s][:, j, :],
                    op0=ALU.mult,
                    op1=ALU.add,
                    accum_out=sums[:, j : j + 1],
                )
            residual[s] = r
            row_sum[s] = sums

        def statistics(s):
            minus = stats.tile([P, TILES], F32, tag="neg_mean")
            nc.scalar.mul(out=minus[:], in_=row_sum[s][:], mul=-1.0 / D)
            squares = work.tile([P, TILES, D], BF16, tag="squares", bufs=1)
            sum_sq = stats.tile([P, TILES], F32, tag="sum_sq")
            for j in range(TILES):
                nc.scalar.activation(
                    out=squares[:, j, :],
                    in_=residual[s][:, j, :],
                    func=ACT.Square,
                    bias=minus[:, j : j + 1],
                    scale=1.0,
                    accum_out=sum_sq[:, j : j + 1],
                )
            root = stats.tile([P, TILES], F32, tag="std")
            nc.scalar.activation(out=root[:], in_=sum_sq[:], func=ACT.Sqrt, bias=eps[:], scale=1.0 / D)
            neg_mean[s] = minus
            std[s] = root

        def inverse_std(s):
            inverse = stats.tile([P, TILES], F32, tag="rstd")
            nc.vector.reciprocal(out=inverse[:], in_=std[s][:])
            rstd[s] = inverse

        def normalise(s):
            for j in range(TILES):
                nc.gpsimd.tensor_scalar(
                    out=residual[s][:, j, :],
                    in0=residual[s][:, j, :],
                    scalar1=neg_mean[s][:, j : j + 1],
                    scalar2=rstd[s][:, j : j + 1],
                    op0=ALU.add,
                    op1=ALU.mult,
                )

        def m_transpose(s):
            planes = work.tile([P, PACK, T], BF16, tag="planes")
            for c in range(PACK):
                bank = ps_t.tile([P, TILES, P], F32, tag="t")
                for j in range(TILES):
                    nc.tensor.transpose(bank[:, j, :], residual[s][:, j, c * P : (c + 1) * P], ident_f32[:])
                nc.scalar.activation(
                    out=planes[:, c, :],
                    in_=bank[:].rearrange("p j t -> p (j t)"),
                    func=ACT.Identity,
                    bias=affine[:, PACK + c : PACK + c + 1],
                    scale=affine[:, c : c + 1],
                )
            m_planes[s] = planes

        def m_quantise(s):
            grouped = work.tile([P, T, PACK], BF16, tag="grouped_m", align_bytes=64)
            nc.vector.tensor_copy(
                out=grouped[:].rearrange("p (w i) c -> p w c i", i=4),
                in_=m_planes[s][:].rearrange("p c (w i) -> p w c i", i=4),
            )
            codes = work.tile([P, T], U32, tag="m_codes", align_bytes=64)
            scales = work.tile([P, T], U8, tag="m_scales", align_bytes=64)
            quantise(grouped, codes, scales)
            m_codes[s] = codes
            m_scales[s] = scales

        def feed_forward(s):
            result = results.tile([P, TILES, F], F32, tag="result")
            out_view = out[s].rearrange("(p j) f -> p j f", j=TILES)
            for j in range(TILES):
                for h in range(F // BANK):
                    acc = ps_mx.tile([P, BANK], F32, tag="mx")
                    nc.tensor.matmul_mx(
                        out=acc[:],
                        lhsT=m_codes[s][:, j * P : (j + 1) * P].bitcast(FP8X4),
                        lhsT_scale=m_scales[s][:, j * P : (j + 1) * P],
                        rhs=ff1_codes[:, h * BANK : (h + 1) * BANK].bitcast(FP8X4),
                        rhs_scale=ff1_scales[:, h * BANK : (h + 1) * BANK],
                        start=True,
                        stop=True,
                    )
                    nc.vector.tensor_tensor(
                        out=result[:, j, h * BANK : (h + 1) * BANK],
                        in0=acc[:],
                        in1=bias_all[:, h * BANK : (h + 1) * BANK],
                        op=ALU.add,
                    )
                nc.scalar.activation(out=result[:, j, :], in_=result[:, j, :], func=ACT.Relu)
                nc.sync.dma_start(out=out_view[:, j, :], in_=result[:, j, :])

        def live(s):
            return 0 <= s < SEQS

        for i in range(-6, SEQS):
            if live(i + 2):
                inverse_std(i + 2)
            if live(i + 4):
                project(i + 4)
            if live(i + 1):
                m_transpose(i + 1)
            if live(i + 6):
                ax_transpose(i + 6)
            if live(i + 2):
                normalise(i + 2)
            if live(i + 5):
                ax_quantise(i + 5)
            if live(i):
                m_quantise(i)
            if live(i + 3):
                statistics(i + 3)
            if i == PREPARE_ROUND:
                prepare_second_layer()
            if live(i):
                feed_forward(i)
